import numpy as np
import ml_dtypes


def mxq(x, axis, fmt="e4m3"):
    dtype, down = {"e4m3": (ml_dtypes.float8_e4m3fn, 7), "e5m2": (ml_dtypes.float8_e5m2, 14)}[fmt]
    v = np.moveaxis(np.asarray(x, np.float32).astype(ml_dtypes.bfloat16).astype(np.float64), axis, -1)
    blocks = v.reshape(v.shape[:-1] + (-1, 32))
    amax = np.abs(blocks).max(-1, keepdims=True)
    byte = np.maximum(np.where(amax > 0, np.frexp(amax)[1] - 1 + 127, 0) - down, 1)
    scale = np.exp2(byte - 127.0)
    codes = (blocks / scale).astype(np.float32).astype(dtype).astype(np.float64)
    return np.moveaxis((codes * scale).reshape(v.shape), -1, axis)


WIDE = False


def mx_kscale(k):
    if not WIDE:
        return np.ones(k)
    levels = np.array([10, -10, 5, -5, 0])
    if k % 512:
        return np.exp2(np.random.permutation(np.resize(levels, k // 32))).repeat(32)
    a = np.empty((k // 512, 16))
    for p in range(k // 512):
        a[p, :8] = np.random.permutation(np.resize(levels, 8))
        for g in range(8):
            far = levels[np.abs(levels - a[p, g]) >= 10]
            a[p, g + 8] = far[np.random.randint(len(far))]
    return np.exp2(a.ravel()).repeat(32)


BF16 = ml_dtypes.bfloat16


def bf(x):
    return np.asarray(x, np.float32).astype(BF16)


def f64(x):
    return np.asarray(x).astype(np.float64)


B, N, SIZE, CH = 256, 16, 1024, 512


def sigmoid(v):
    return 1.0 / (1.0 + np.exp(-v))


def draw0():
    s = mx_kscale(SIZE)
    half = np.concatenate([np.ones(CH), np.full(CH, 2.0 / np.sqrt(N))])
    return {"z_node": bf(np.random.standard_normal((B, N, SIZE)) * s),
            "z_children": bf(np.random.standard_normal((B, N, SIZE)) * half),
            "W_f": bf(np.random.standard_normal((CH, SIZE)) / np.sqrt(SIZE) / s),
            "U_f": bf(np.random.standard_normal((CH, CH)) / np.sqrt(CH)),
            "b_f": bf(np.random.standard_normal(CH) * 0.5)}


def core(z_node, z_children, W_f, U_f, b_f):
    h_k = f64(z_children)[..., :CH]
    c_k = f64(z_children)[..., CH:]
    f_j_k = sigmoid((mxq(f64(z_node), 2, "e4m3") @ mxq(f64(W_f), 1, "e4m3").T) + h_k @ f64(U_f).T + f64(b_f))
    return (f_j_k * c_k).sum(axis=1)


def e4m3fn_bytes(y):
    return np.clip(np.asarray(y, np.float64), -448.0, 448.0).astype(np.float32).astype(ml_dtypes.float8_e4m3fn).view(np.uint8)


def e4m3fn_values(b):
    return np.asarray(b, np.uint8).view(ml_dtypes.float8_e4m3fn).astype(np.float64)


def setup_inputs():
    d = draw0()
    x0 = np.asarray(d['z_node']).astype(np.float64)
    s = (np.max(np.abs(x0), axis=(0, 1), keepdims=True) / 448.0).astype(np.float32)
    out = {}
    for k, v in d.items():
        if k == 'z_node':
            out['z_node_bytes'] = e4m3fn_bytes(x0 / s.astype(np.float64))
            out['z_node_scale'] = s
        else:
            out[k] = v
    return out


def reference(z_node_bytes, z_node_scale, z_children, W_f, U_f, b_f):
    return core(e4m3fn_values(z_node_bytes) * z_node_scale.astype(np.float64), z_children, W_f, U_f, b_f)

@@ -1,0 +1,348 @@
+from contextlib import ExitStack
+
+import concourse.masks as masks
+import concourse.mybir as mybir
+
+PIN = "all"
+WEAVE = True
+
+F32 = mybir.dt.float32
+BF16 = mybir.dt.bfloat16
+U32 = mybir.dt.uint32
+U8 = mybir.dt.uint8
+FP8 = mybir.dt.float8_e4m3fn
+FP8X4 = mybir.dt.float8_e4m3fn_x4
+ALU = mybir.AluOpType
+ACT = mybir.ActivationFunctionType
+
+P = 128
+NODES, KIDS, SIZE, CH = 256, 16, 1024, 512
+TOKENS = NODES * KIDS
+FLOPS = 2 * TOKENS * CH * (SIZE + CH)
+
+GROUP = 512
+N_GROUPS = TOKENS // GROUP
+N_STEPS = 4 * N_GROUPS
+LW = 9
+LZ = 7
+LP = 3
+LH = LP + 4
+GL = 2
+U_AT = -4
+W_AT = -4
+WQ_AT = -3
+HEAD = "scale z0s c0s z1 U W b z2 c1 z3 c2 c3"
+Z_BUFS = 4
+C_BUFS = 4
+
+
+def tile_treelstm_pa_kernel(tc, z_node_bytes, z_node_scale, z_children, W_f, U_f, b_f, out):
+    nc = tc.nc
+
+    with ExitStack() as ctx:
+        const = ctx.enter_context(tc.tile_pool(name="const", bufs=1))
+        loads = ctx.enter_context(tc.tile_pool(name="loads", bufs=4))
+        work = ctx.enter_context(tc.tile_pool(name="work", bufs=2))
+        psum = ctx.enter_context(tc.psum_pool(name="psum", bufs=2))
+
+        ident_f = const.tile([P, P], F32, name="ident_f", tag="ident_f")
+        masks.make_identity(nc, ident_f[:])
+        ident_b = const.tile([P, P], BF16, name="ident_b", tag="ident_b")
+        masks.make_identity(nc, ident_b[:])
+        warm_in = const.tile([P, 1], F32, name="warm_in", tag="warm_in")
+        warm_out = const.tile([P, 1], F32, name="warm_out", tag="warm_out")
+        nc.vector.memset(warm_in[:], 0.0)
+        nc.scalar.activation(out=warm_out[:], in_=warm_in[:], func=ACT.Sigmoid)
+
+        scale_bc = const.tile([P, SIZE], F32, name="scale_bc", tag="scale_bc")
+        w_sb = const.tile([P, 4, SIZE], BF16, name="w_sb", tag="w_sb")
+        u_sb = const.tile([P, 4, CH], BF16, name="u_sb", tag="u_sb")
+        bias = const.tile([P, 4], BF16, name="bias", tag="bias")
+        w_grp = const.tile([P, 2, CH, 4], BF16, name="w_grp", tag="w_grp", align_bytes=64)
+        w_q = const.tile([P, 2, CH], U32, name="w_q", tag="w_q", align_bytes=64)
+        w_s = const.tile([P, 2, CH], U8, name="w_s", tag="w_s", align_bytes=64)
+        u_t = const.tile([P, 4, CH], BF16, name="u_t", tag="u_t")
+
+
+        zby = {}
+        chd = {}
+        zbt = {}
+        grp = {}
+        h_t = {}
+        c_t = {}
+        z_q = {}
+        z_s = {}
+        pl_b = {}
+        mx_b = {}
+        pp_t = {}
+        x_t = {}
+        f_t = {}
+        g_t = {}
+        acc = {}
+
+        def load_rows(src3, t, g, split):
+            hb, gam = divmod(g, 4)
+            src = src3[P * hb:P * (hb + 1), 4 * gam:4 * (gam + 1), :]
+            if split:
+                for j in range(4):
+                    nc.sync.dma_start(out=t[:, j, :], in_=src[:, j, :])
+            else:
+                nc.sync.dma_start(out=t[:], in_=src)
+
+        def load_bytes(g, split):
+            zby[g] = loads.tile([P, 4, SIZE], U8, name="zbytes", tag="zbytes", bufs=Z_BUFS)
+            load_rows(z_node_bytes, zby[g], g, split)
+
+        def load_children(g, split):
+            chd[g] = loads.tile([P, 4, SIZE], BF16, name="child", tag="child", bufs=C_BUFS)
+            load_rows(z_children, chd[g], g, split)
+
+        def widen(x):
+            g, j = divmod(x, 4)
+            t = work.tile([P, SIZE], BF16, name="zb", tag="zb", bufs=LW - LZ + 4)
+            nc.vector.tensor_tensor(out=t[:], in0=zby[g][:, j, :].bitcast(FP8), in1=scale_bc[:], op=ALU.mult)
+            zbt[x] = t
+
+        def words_parts(src, dst, col):
+            zt = psum.tile([P, 2, 2, P], F32, name="zt", tag="zt")
+            words = src.bitcast(F32)
+
+            def one(g, u):
+                return lambda: nc.tensor.transpose(zt[:, g, u, :], words[:, 256 * g + u:256 * (g + 1):2], ident_f[:])
+
+            def leave():
+                dst_words = dst[:].rearrange("p g t k -> p (g t k)").bitcast(F32).rearrange("p (g t u) -> p g t u", g=2, u=2)
+                nc.scalar.copy(out=dst_words[:, :, P * col:P * (col + 1), :], in_=zt[:].rearrange("p g u r -> p g r u"))
+
+            return [one(g, u) for g in range(2) for u in range(2)], leave
+
+        def u_bank_parts(h_src, h_dst, col):
+            hc = psum.tile([P, 512], F32, name="hc", tag="hc", bufs=1)
+            hv = hc[:, 0:256].bitcast(BF16).rearrange("p (kt r) -> p kt r", kt=4)
+
+            def one_h(kt):
+                return lambda: nc.tensor.transpose(hv[:, kt, :], h_src[:, P * kt:P * (kt + 1)], ident_b[:])
+
+            def leave_h():
+                nc.scalar.copy(out=h_dst[:, :, P * col:P * (col + 1)], in_=hv)
+
+            return [one_h(kt) for kt in range(4)], [leave_h]
+
+        def hc_bank_parts(h_src, c_src, dst, col):
+            hc = psum.tile([P, 512], F32, name="hc", tag="hc", bufs=1)
+            hv = hc[:, 0:256].bitcast(BF16).rearrange("p (kt r) -> p kt r", kt=4)
+            words = c_src.bitcast(F32)
+
+            def one_h(kt):
+                return lambda: nc.tensor.transpose(hv[:, kt, :], h_src[:, P * kt:P * (kt + 1)], ident_b[:])
+
+            def one_c(q):
+                return lambda: nc.tensor.transpose(hc[:, 256 + P * q:256 + P * (q + 1)], words[:, P * q:P * (q + 1)], ident_f[:])
+
+            def leave():
+                dst_words = dst[:].rearrange("p i j r -> p (i j r)").bitcast(F32).rearrange("p (i j w) -> p i j w", i=8, j=4)
+                nc.scalar.copy(out=dst_words[:, :, col, :], in_=hc[:].rearrange("p (i w) -> p i w", i=8))
+
+            return [one_h(kt) for kt in range(4)] + [one_c(q) for q in range(2)], [leave]
+
+        def z_parts(x):
+            g, j = divmod(x, 4)
+            if j == 0:
+                grp[g] = work.tile([P, 2, GROUP, 4], BF16, name="grp", tag="grp", align_bytes=64)
+            return words_parts(zbt[x][:], grp[g], j)
+
+        def hc_parts(x):
+            g, j = divmod(x, 4)
+            if j == 0:
+                h_t[g] = work.tile([P, 8, 4, P], BF16, name="hc_t", tag="hc_t", bufs=(LH + 7) // 4 + 2)
+            return hc_bank_parts(chd[g][:, j, 0:CH], chd[g][:, j, CH:SIZE], h_t[g], j)
+
+        def quantize(src, codes, scales):
+            nc.vector.quantize_mx(
+                out=codes[:].rearrange("p g t -> p (g t)").bitcast(FP8X4),
+                scales=scales[:].rearrange("p g t -> p (g t)"),
+                in_=src[:].rearrange("p g t k -> p (g t k)"),
+            )
+
+        def quant(g):
+            z_q[g] = work.tile([P, 2, GROUP], U32, name="z_q", tag="z_q", align_bytes=64)
+            z_s[g] = work.tile([P, 2, GROUP], U8, name="z_s", tag="z_s", align_bytes=64)
+            quantize(grp[g], z_q[g], z_s[g])
+
+        def p_parts(s):
+            g, a = divmod(s, 4)
+            t = psum.tile([P, GROUP], F32, name="pl", tag="pl")
+            pl_b[s] = t
+
+            def one(kt):
+                return lambda: nc.tensor.matmul(t[:], lhsT=u_t[:, kt, P * a:P * (a + 1)], rhs=h_t[g][:, kt, :, :].rearrange("p j r -> p (j r)"), start=(kt == 0), stop=(kt == 3))
+
+            return [one(kt) for kt in range(4)]
+
+        def mxmm(s):
+            g, a = divmod(s, 4)
+            t = psum.tile([P, GROUP], F32, name="mx", tag="mx")
+            for c in range(2):
+                nc.tensor.matmul_mx(
+                    out=t[:],
+                    lhsT=w_q[:, c, P * a:P * (a + 1)].bitcast(FP8X4),
+                    lhsT_scale=w_s[:, c, P * a:P * (a + 1)],
+                    rhs=z_q[g][:, c, :].bitcast(FP8X4),
+                    rhs_scale=z_s[g][:, c, :],
+                    start=(c == 0),
+                    stop=(c == 1),
+                )
+            mx_b[s] = t
+
+        def plain_out(s):
+            t = work.tile([P, GROUP], F32, name="pp", tag="pp", bufs=LP + 2)
+            nc.scalar.copy(out=t[:], in_=pl_b[s][:])
+            pp_t[s] = t
+
+        def add(s):
+            t = work.tile([P, GROUP], F32, name="x", tag="x")
+            nc.vector.tensor_tensor(out=t[:], in0=mx_b[s][:], in1=pp_t[s][:], op=ALU.add)
+            x_t[s] = t
+
+        def sig(s):
+            t = work.tile([P, GROUP], F32, name="f", tag="f", bufs=3)
+            nc.scalar.activation(out=t[:], in_=x_t[s][:], func=ACT.Sigmoid, bias=bias[:, s % 4:s % 4 + 1], scale=1.0)
+            f_t[s] = t
+
+        def mul(s):
+            g, a = divmod(s, 4)
+            q, e = divmod(a, 2)
+            t = work.tile([P, GROUP], F32, name="gm", tag="gm", bufs=GL + 2)
+            cells = h_t[g][:, 4 + 2 * q:6 + 2 * q, :, :].rearrange("p h j (r e) -> p j h r e", e=2)[:, :, :, :, e]
+            nc.vector.tensor_tensor(
+                out=t[:].rearrange("p (j h r) -> p j h r", j=4, h=2),
+                in0=f_t[s][:].rearrange("p (j h r) -> p j h r", j=4, h=2),
+                in1=cells,
+                op=ALU.mult,
+            )
+            g_t[s] = t
+
+        def sum_parts(s):
+            g, a = divmod(s, 4)
+            hb = g // 4
+            if s % 16 == 0:
+                acc[hb] = psum.tile([P, 4, P], F32, name="acc", tag="acc", bufs=1)
+
+            def one(j):
+                return lambda: nc.tensor.matmul(
+                    acc[hb][:, a, :],
+                    lhsT=g_t[s][:, P * j:P * (j + 1)],
+                    rhs=ident_f[:],
+                    is_transpose=True,
+                    start=(s % 16 == 0 and j == 0),
+                    stop=(s % 16 == 15 and j == 3),
+                )
+
+            return [one(j) for j in range(4)]
+
+        def store_half(hb):
+            osb = work.tile([P, CH], F32, name="osb", tag="osb")
+            nc.scalar.copy(
+                out=osb[:].rearrange("p (q w e) -> p q w e", q=2, e=2),
+                in_=acc[hb][:].rearrange("p (q e) w -> p q w e", q=2),
+            )
+            nc.sync.dma_start(out=out[P * hb:P * (hb + 1), :], in_=osb[:])
+
+        loaded = set()
+        for tok in HEAD.split(" "):
+            if tok == "scale":
+                nc.sync.dma_start(out=scale_bc[:], in_=z_node_scale.rearrange("a b k -> (a b k)").partition_broadcast(P))
+            elif tok == "W":
+                nc.sync.dma_start(
+                    out=w_sb[:].rearrange("m (q e) k -> m q (e k)", q=2),
+                    in_=W_f.rearrange("(q m e) k -> m q (e k)", q=2, m=P, e=2),
+                )
+            elif tok == "U":
+                nc.sync.dma_start(
+                    out=u_sb[:].rearrange("m (q e) k -> m q (e k)", q=2),
+                    in_=U_f.rearrange("(q m e) k -> m q (e k)", q=2, m=P, e=2),
+                )
+            elif tok == "b":
+                with nc.allow_non_contiguous_dma(reason="the bias, two neighbouring channels to a partition"):
+                    nc.sync.dma_start(
+                        out=bias[:].rearrange("m (q e) -> m q e", q=2),
+                        in_=b_f.rearrange("(q m e) -> m q e", q=2, m=P, e=2),
+                    )
+            elif tok.startswith("z"):
+                load_bytes(int(tok[1]), len(tok) > 2)
+                loaded.add(tok[0:2])
+            else:
+                load_children(int(tok[1]), len(tok) > 2)
+                loaded.add(tok[0:2])
+
+        for s in range(-max(LW, LH) - 1, N_STEPS + GL + 1):
+            if PIN == "pe" and s == -1:
+                ctx.enter_context(tc.manual_schedule(engines={mybir.EngineType.PE}))
+            if PIN == "all" and s == -1:
+                ctx.enter_context(tc.manual_schedule())
+            for g in range(N_GROUPS):
+                if "z" + str(g) not in loaded and s >= 4 * (g - Z_BUFS) + 4 - LW:
+                    load_bytes(g, False)
+                    loaded.add("z" + str(g))
+                if "c" + str(g) not in loaded and s >= 4 * (g - C_BUFS) + 4 - LH:
+                    load_children(g, False)
+                    loaded.add("c" + str(g))
+            if 0 <= s < N_STEPS:
+                add(s)
+                sig(s)
+            if 0 <= s + LW < N_STEPS:
+                widen(s + LW)
+            if 0 <= s - 1 < N_STEPS:
+                mul(s - 1)
+            if (s + 3) % 4 == 0 and 0 <= (s + 3) // 4 < N_GROUPS:
+                quant((s + 3) // 4)
+            if s == WQ_AT:
+                quantize(w_grp, w_q, w_s)
+            if 0 <= s + LP - 1 < N_STEPS:
+                plain_out(s + LP - 1)
+            if 0 <= s + 2 < N_STEPS:
+                mxmm(s + 2)
+            if s == U_AT:
+                for a in range(4):
+                    fs, las = u_bank_parts(u_sb[:, a, :], u_t, a)
+                    for f in fs:
+                        f()
+                    las[0]()
+            if s == W_AT:
+                for a in range(4):
+                    fs, la = words_parts(w_sb[:, a, :], w_grp, a)
+                    for f in fs:
+                        f()
+                    la()
+            zs = []
+            hcs = []
+            gs = []
+            leaves = []
+            if 0 <= s + LH < N_STEPS:
+                hcs, las = hc_parts(s + LH)
+                leaves.extend(las)
+            if 0 <= s + LZ < N_STEPS:
+                zs, la = z_parts(s + LZ)
+                leaves.append(la)
+            if 0 <= s - GL < N_STEPS:
+                gs = sum_parts(s - GL)
+            ps = p_parts(s + LP) if 0 <= s + LP < N_STEPS else []
+            if WEAVE and len(ps) > 0:
+                gaps = [
+                    zs[0:1] + hcs[0:2] + hcs[4:5] + gs[0:1],
+                    zs[1:2] + hcs[2:4] + hcs[5:6] + gs[1:2],
+                    zs[2:4] + gs[2:4],
+                ]
+                for n in range(4):
+                    ps[n]()
+                    if n < 3:
+                        for f in gaps[n]:
+                            f()
+            else:
+                for f in zs + hcs + gs + ps:
+                    f()
+            for la in leaves:
+                la()
+            if s == 15 + GL:
+                store_half(0)
+        store_half(1)

@@ -3,8 +3,8 @@ from contextlib import ExitStack
 import concourse.masks as masks
 import concourse.mybir as mybir
 
-PIN = "all"
 WEAVE = True
+N_WARM = 4
 
 F32 = mybir.dt.float32
 BF16 = mybir.dt.bfloat16
@@ -25,13 +25,13 @@ N_GROUPS = TOKENS // GROUP
 N_STEPS = 4 * N_GROUPS
 LW = 9
 LZ = 7
-LP = 3
+LP = 6
 LH = LP + 4
 GL = 2
 U_AT = -4
 W_AT = -4
 WQ_AT = -3
-HEAD = "scale z0s c0s z1 U W b z2 c1 z3 c2 c3"
+HEAD = "c00 c01 U c02 c03 W0 scale z00 W1 z01 z02 z03 b c1 z1 z2 c2 z3 c3"
 Z_BUFS = 4
 C_BUFS = 4
 
@@ -45,12 +45,15 @@ def tile_treelstm_pa_kernel(tc, z_node_bytes, z_node_scale, z_children, W_f, U_f
         work = ctx.enter_context(tc.tile_pool(name="work", bufs=2))
         psum = ctx.enter_context(tc.psum_pool(name="psum", bufs=2))
 
+        ctx.enter_context(tc.manual_schedule())
         ident_f = const.tile([P, P], F32, name="ident_f", tag="ident_f")
         masks.make_identity(nc, ident_f[:])
         ident_b = const.tile([P, P], BF16, name="ident_b", tag="ident_b")
         masks.make_identity(nc, ident_b[:])
         warm_in = const.tile([P, 1], F32, name="warm_in", tag="warm_in")
         warm_out = const.tile([P, 1], F32, name="warm_out", tag="warm_out")
+        idle_in = const.tile([P, GROUP], BF16, name="idle_in", tag="idle_in")
+        nc.vector.memset(idle_in[:], 0.0)
         nc.vector.memset(warm_in[:], 0.0)
         nc.scalar.activation(out=warm_out[:], in_=warm_in[:], func=ACT.Sigmoid)
 
@@ -80,22 +83,33 @@ def tile_treelstm_pa_kernel(tc, z_node_bytes, z_node_scale, z_children, W_f, U_f
         g_t = {}
         acc = {}
 
-        def load_rows(src3, t, g, split):
+        def load_rows(src3, t, g, piece):
             hb, gam = divmod(g, 4)
             src = src3[P * hb:P * (hb + 1), 4 * gam:4 * (gam + 1), :]
-            if split:
-                for j in range(4):
-                    nc.sync.dma_start(out=t[:, j, :], in_=src[:, j, :])
-            else:
+            if piece is None:
                 nc.sync.dma_start(out=t[:], in_=src)
+            else:
+                nc.sync.dma_start(out=t[:, piece, :], in_=src[:, piece, :])
 
-        def load_bytes(g, split):
-            zby[g] = loads.tile([P, 4, SIZE], U8, name="zbytes", tag="zbytes", bufs=Z_BUFS)
-            load_rows(z_node_bytes, zby[g], g, split)
+        def load_bytes(g, piece):
+            if g not in zby:
+                zby[g] = loads.tile([P, 4, SIZE], U8, name="zbytes", tag="zbytes", bufs=Z_BUFS)
+            load_rows(z_node_bytes, zby[g], g, piece)
 
-        def load_children(g, split):
-            chd[g] = loads.tile([P, 4, SIZE], BF16, name="child", tag="child", bufs=C_BUFS)
-            load_rows(z_children, chd[g], g, split)
+        def load_children(g, piece):
+            if g not in chd:
+                chd[g] = loads.tile([P, 4, SIZE], BF16, name="child", tag="child", bufs=C_BUFS)
+            load_rows(z_children, chd[g], g, piece)
+
+        def move(eng, out, in_):
+            if eng == "V":
+                nc.vector.tensor_copy(out=out, in_=in_)
+            else:
+                nc.scalar.copy(out=out, in_=in_)
+
+        def idle_pass():
+            t = psum.tile([P, GROUP], F32, name="pl", tag="pl")
+            nc.tensor.matmul(t[:], lhsT=idle_in[:, 0:P], rhs=idle_in[:], start=True, stop=True)
 
         def widen(x):
             g, j = divmod(x, 4)
@@ -117,19 +131,19 @@ def tile_treelstm_pa_kernel(tc, z_node_bytes, z_node_scale, z_children, W_f, U_f
             return [one(g, u) for g in range(2) for u in range(2)], leave
 
         def u_bank_parts(h_src, h_dst, col):
-            hc = psum.tile([P, 512], F32, name="hc", tag="hc", bufs=1)
+            hc = psum.tile([P, 512], F32, name="zt", tag="zt")
             hv = hc[:, 0:256].bitcast(BF16).rearrange("p (kt r) -> p kt r", kt=4)
 
             def one_h(kt):
                 return lambda: nc.tensor.transpose(hv[:, kt, :], h_src[:, P * kt:P * (kt + 1)], ident_b[:])
 
             def leave_h():
-                nc.scalar.copy(out=h_dst[:, :, P * col:P * (col + 1)], in_=hv)
+                move("V", h_dst[:, :, P * col:P * (col + 1)], hv)
 
             return [one_h(kt) for kt in range(4)], [leave_h]
 
-        def hc_bank_parts(h_src, c_src, dst, col):
-            hc = psum.tile([P, 512], F32, name="hc", tag="hc", bufs=1)
+        def hc_bank_parts(h_src, c_src, dst, col, tag, eng):
+            hc = psum.tile([P, 512], F32, name=tag, tag=tag, bufs=(1 if tag == "hc" else 2))
             hv = hc[:, 0:256].bitcast(BF16).rearrange("p (kt r) -> p kt r", kt=4)
             words = c_src.bitcast(F32)
 
@@ -141,7 +155,7 @@ def tile_treelstm_pa_kernel(tc, z_node_bytes, z_node_scale, z_children, W_f, U_f
 
             def leave():
                 dst_words = dst[:].rearrange("p i j r -> p (i j r)").bitcast(F32).rearrange("p (i j w) -> p i j w", i=8, j=4)
-                nc.scalar.copy(out=dst_words[:, :, col, :], in_=hc[:].rearrange("p (i w) -> p i w", i=8))
+                move(eng, dst_words[:, :, col, :], hc[:].rearrange("p (i w) -> p i w", i=8))
 
             return [one_h(kt) for kt in range(4)] + [one_c(q) for q in range(2)], [leave]
 
@@ -151,11 +165,11 @@ def tile_treelstm_pa_kernel(tc, z_node_bytes, z_node_scale, z_children, W_f, U_f
                 grp[g] = work.tile([P, 2, GROUP, 4], BF16, name="grp", tag="grp", align_bytes=64)
             return words_parts(zbt[x][:], grp[g], j)
 
-        def hc_parts(x):
+        def hc_parts(x, tag="hc", eng="S"):
             g, j = divmod(x, 4)
             if j == 0:
                 h_t[g] = work.tile([P, 8, 4, P], BF16, name="hc_t", tag="hc_t", bufs=(LH + 7) // 4 + 2)
-            return hc_bank_parts(chd[g][:, j, 0:CH], chd[g][:, j, CH:SIZE], h_t[g], j)
+            return hc_bank_parts(chd[g][:, j, 0:CH], chd[g][:, j, CH:SIZE], h_t[g], j, tag, eng)
 
         def quantize(src, codes, scales):
             nc.vector.quantize_mx(
@@ -252,10 +266,11 @@ def tile_treelstm_pa_kernel(tc, z_node_bytes, z_node_scale, z_children, W_f, U_f
         for tok in HEAD.split(" "):
             if tok == "scale":
                 nc.sync.dma_start(out=scale_bc[:], in_=z_node_scale.rearrange("a b k -> (a b k)").partition_broadcast(P))
-            elif tok == "W":
+            elif tok.startswith("W"):
+                q = int(tok[1])
                 nc.sync.dma_start(
-                    out=w_sb[:].rearrange("m (q e) k -> m q (e k)", q=2),
-                    in_=W_f.rearrange("(q m e) k -> m q (e k)", q=2, m=P, e=2),
+                    out=w_sb[:, 2 * q:2 * q + 2, :].rearrange("m e k -> m (e k)"),
+                    in_=W_f.rearrange("(q m e) k -> q m (e k)", q=2, m=P, e=2)[q],
                 )
             elif tok == "U":
                 nc.sync.dma_start(
@@ -269,23 +284,87 @@ def tile_treelstm_pa_kernel(tc, z_node_bytes, z_node_scale, z_children, W_f, U_f
                         in_=b_f.rearrange("(q m e) -> m q e", q=2, m=P, e=2),
                     )
             elif tok.startswith("z"):
-                load_bytes(int(tok[1]), len(tok) > 2)
+                load_bytes(int(tok[1]), int(tok[2]) if len(tok) > 2 else None)
                 loaded.add(tok[0:2])
             else:
-                load_children(int(tok[1]), len(tok) > 2)
+                load_children(int(tok[1]), int(tok[2]) if len(tok) > 2 else None)
                 loaded.add(tok[0:2])
 
-        for s in range(-max(LW, LH) - 1, N_STEPS + GL + 1):
-            if PIN == "pe" and s == -1:
-                ctx.enter_context(tc.manual_schedule(engines={mybir.EngineType.PE}))
-            if PIN == "all" and s == -1:
-                ctx.enter_context(tc.manual_schedule())
+        done = set()
+
+        def run(parts):
+            for f in parts:
+                f()
+
+        def turn_hc(x, tag, eng):
+            fs, las = hc_parts(x, tag, eng)
+            run(fs)
+            run(las)
+            done.add(("hc", x))
+
+        def turn_u(a):
+            fs, las = u_bank_parts(u_sb[:, a, :], u_t, a)
+            run(fs)
+            run(las)
+
+        def plain_round(s, groups):
+            ps = p_parts(s)
+            for n in range(4):
+                ps[n]()
+                if n < len(groups):
+                    fs, la = groups[n]()
+                    run(fs)
+                    la()
+            plain_out(s)
+            done.add(("p", s))
+            done.add(("pp", s))
+
+        def w_group(a):
+            return lambda: words_parts(w_sb[:, a, :], w_grp, a)
+
+        def z_group(x):
+            done.add(("z", x))
+            return lambda: z_parts(x)
+
+        for n in range(N_WARM):
+            idle_pass()
+        turn_hc(0, "hc", "V")
+        turn_hc(1, "mx", "V")
+        idle_pass()
+        for a in range(4):
+            turn_u(a)
+        idle_pass()
+        turn_hc(2, "mx", "V")
+        turn_hc(3, "hc", "V")
+        idle_pass()
+        widen(0)
+        plain_round(0, [w_group(0)])
+        widen(1)
+        plain_round(1, [w_group(1)])
+        widen(2)
+        plain_round(2, [w_group(2), w_group(3)])
+        widen(3)
+        quantize(w_grp, w_q, w_s)
+        plain_round(3, [z_group(0), z_group(1), z_group(2), z_group(3)])
+        widen(4)
+        turn_hc(4, "hc", "S")
+        fs, la = z_group(4)()
+        run(fs)
+        la()
+        quant(0)
+        turn_hc(5, "mx", "S")
+        turn_hc(6, "mx", "S")
+        widen(5)
+        turn_hc(7, "hc", "S")
+        widen(6)
+
+        for s in range(-2, N_STEPS + GL + 1):
             for g in range(N_GROUPS):
                 if "z" + str(g) not in loaded and s >= 4 * (g - Z_BUFS) + 4 - LW:
-                    load_bytes(g, False)
+                    load_bytes(g, None)
                     loaded.add("z" + str(g))
                 if "c" + str(g) not in loaded and s >= 4 * (g - C_BUFS) + 4 - LH:
-                    load_children(g, False)
+                    load_children(g, None)
                     loaded.add("c" + str(g))
             if 0 <= s < N_STEPS:
                 add(s)
@@ -296,37 +375,23 @@ def tile_treelstm_pa_kernel(tc, z_node_bytes, z_node_scale, z_children, W_f, U_f
                 mul(s - 1)
             if (s + 3) % 4 == 0 and 0 <= (s + 3) // 4 < N_GROUPS:
                 quant((s + 3) // 4)
-            if s == WQ_AT:
-                quantize(w_grp, w_q, w_s)
-            if 0 <= s + LP - 1 < N_STEPS:
+            if 0 <= s + LP - 1 < N_STEPS and ("pp", s + LP - 1) not in done:
                 plain_out(s + LP - 1)
             if 0 <= s + 2 < N_STEPS:
                 mxmm(s + 2)
-            if s == U_AT:
-                for a in range(4):
-                    fs, las = u_bank_parts(u_sb[:, a, :], u_t, a)
-                    for f in fs:
-                        f()
-                    las[0]()
-            if s == W_AT:
-                for a in range(4):
-                    fs, la = words_parts(w_sb[:, a, :], w_grp, a)
-                    for f in fs:
-                        f()
-                    la()
             zs = []
             hcs = []
             gs = []
             leaves = []
-            if 0 <= s + LH < N_STEPS:
+            if 0 <= s + LH < N_STEPS and ("hc", s + LH) not in done:
                 hcs, las = hc_parts(s + LH)
                 leaves.extend(las)
-            if 0 <= s + LZ < N_STEPS:
+            if 0 <= s + LZ < N_STEPS and ("z", s + LZ) not in done:
                 zs, la = z_parts(s + LZ)
                 leaves.append(la)
             if 0 <= s - GL < N_STEPS:
                 gs = sum_parts(s - GL)
-            ps = p_parts(s + LP) if 0 <= s + LP < N_STEPS else []
+            ps = p_parts(s + LP) if 0 <= s + LP < N_STEPS and ("p", s + LP) not in done else []
             if WEAVE and len(ps) > 0:
                 gaps = [
                     zs[0:1] + hcs[0:2] + hcs[4:5] + gs[0:1],

@@ -23,8 +23,8 @@ FLOPS = 2 * TOKENS * CH * (SIZE + CH)
 GROUP = 512
 N_GROUPS = TOKENS // GROUP
 N_STEPS = 4 * N_GROUPS
-LW = 9
-LZ = 7
+LW = 10
+LZ = 8
 LP = 6
 LH = LP + 4
 GL = 2
@@ -356,7 +356,11 @@ def tile_treelstm_pa_kernel(tc, z_node_bytes, z_node_scale, z_children, W_f, U_f
         turn_hc(6, "mx", "S")
         widen(5)
         turn_hc(7, "hc", "S")
+        fs, la = z_group(5)()
+        run(fs)
+        la()
         widen(6)
+        widen(7)
 
         for s in range(-2, N_STEPS + GL + 1):
             for g in range(N_GROUPS):

@@ -4,7 +4,14 @@ import concourse.masks as masks
 import concourse.mybir as mybir
 
 WEAVE = True
-N_WARM = 4
+HEAD_ORDER = """
+D D D D H0/hc/V H1/mx/V D U0/V U1/V D H2/mx/S H3/hc/S W0/S W1/S w0
+w1 p0 p0 p0 p0 c0
+w2 w3 p1 Z0/S/mx p1 W2/S p1 W3/S p1 c1
+qW p2 Z1/S/mx p2 Z2 p2 Z3 p2 c2
+w4 q0 p3 H4/hc/S p3 H5/mx/S p3 p3 c3
+w5 w6 H6/mx/S Z4 H7/hc/S w7 Z5
+"""
 
 F32 = mybir.dt.float32
 BF16 = mybir.dt.bfloat16
@@ -27,7 +34,7 @@ LW = 10
 LZ = 8
 LP = 6
 LH = LP + 4
-GL = 2
+GL = 3
 U_AT = -4
 W_AT = -4
 WQ_AT = -3
@@ -117,8 +124,8 @@ def tile_treelstm_pa_kernel(tc, z_node_bytes, z_node_scale, z_children, W_f, U_f
             nc.vector.tensor_tensor(out=t[:], in0=zby[g][:, j, :].bitcast(FP8), in1=scale_bc[:], op=ALU.mult)
             zbt[x] = t
 
-        def words_parts(src, dst, col):
-            zt = psum.tile([P, 2, 2, P], F32, name="zt", tag="zt")
+        def words_parts(src, dst, col, eng="S", tag="zt"):
+            zt = psum.tile([P, 2, 2, P], F32, name=tag, tag=tag, bufs=(1 if tag in ("hc", "acc") else 2))
             words = src.bitcast(F32)
 
             def one(g, u):
@@ -126,21 +133,25 @@ def tile_treelstm_pa_kernel(tc, z_node_bytes, z_node_scale, z_children, W_f, U_f
 
             def leave():
                 dst_words = dst[:].rearrange("p g t k -> p (g t k)").bitcast(F32).rearrange("p (g t u) -> p g t u", g=2, u=2)
-                nc.scalar.copy(out=dst_words[:, :, P * col:P * (col + 1), :], in_=zt[:].rearrange("p g u r -> p g r u"))
+                move(eng, dst_words[:, :, P * col:P * (col + 1), :], zt[:].rearrange("p g u r -> p g r u"))
 
             return [one(g, u) for g in range(2) for u in range(2)], leave
 
-        def u_bank_parts(h_src, h_dst, col):
-            hc = psum.tile([P, 512], F32, name="zt", tag="zt")
-            hv = hc[:, 0:256].bitcast(BF16).rearrange("p (kt r) -> p kt r", kt=4)
+        def u_bank_parts(pair, eng):
+            ub = psum.tile([P, 512], F32, name="zt", tag="zt")
+            uv = ub[:].bitcast(BF16).rearrange("p (a kt m) -> p a kt m", a=2, kt=4)
 
-            def one_h(kt):
-                return lambda: nc.tensor.transpose(hv[:, kt, :], h_src[:, P * kt:P * (kt + 1)], ident_b[:])
+            def one(a, kt):
+                return lambda: nc.tensor.transpose(uv[:, a, kt, :], u_sb[:, 2 * pair + a, P * kt:P * (kt + 1)], ident_b[:])
 
-            def leave_h():
-                move("V", h_dst[:, :, P * col:P * (col + 1)], hv)
+            def leave():
+                move(
+                    eng,
+                    u_t[:, :, 2 * P * pair:2 * P * (pair + 1)].rearrange("p kt (a m) -> p kt a m", a=2),
+                    uv.rearrange("p a kt m -> p kt a m"),
+                )
 
-            return [one_h(kt) for kt in range(4)], [leave_h]
+            return [one(a, kt) for a in range(2) for kt in range(4)], [leave]
 
         def hc_bank_parts(h_src, c_src, dst, col, tag, eng):
             hc = psum.tile([P, 512], F32, name=tag, tag=tag, bufs=(1 if tag == "hc" else 2))
@@ -159,11 +170,11 @@ def tile_treelstm_pa_kernel(tc, z_node_bytes, z_node_scale, z_children, W_f, U_f
 
             return [one_h(kt) for kt in range(4)] + [one_c(q) for q in range(2)], [leave]
 
-        def z_parts(x):
+        def z_parts(x, eng="S", tag="zt"):
             g, j = divmod(x, 4)
             if j == 0:
                 grp[g] = work.tile([P, 2, GROUP, 4], BF16, name="grp", tag="grp", align_bytes=64)
-            return words_parts(zbt[x][:], grp[g], j)
+            return words_parts(zbt[x][:], grp[g], j, eng, tag)
 
         def hc_parts(x, tag="hc", eng="S"):
             g, j = divmod(x, 4)
@@ -296,71 +307,71 @@ def tile_treelstm_pa_kernel(tc, z_node_bytes, z_node_scale, z_children, W_f, U_f
             for f in parts:
                 f()
 
-        def turn_hc(x, tag, eng):
-            fs, las = hc_parts(x, tag, eng)
-            run(fs)
-            run(las)
-            done.add(("hc", x))
+        open_p = {}
+        for tok in HEAD_ORDER.split():
+            f = tok.split("/")
+            k = f[0][0]
+            n = int(f[0][1:]) if len(f[0]) > 1 and f[0][1:] != "W" else 0
+            if (k == "H" and n >= LH - 2) or (k == "Z" and n >= LZ - 2) or (k in ("p", "c") and n >= LP - 2) or (k == "w" and n >= LW - 2):
+                continue
+            if tok == "D":
+                idle_pass()
+            elif k == "H":
+                fs, las = hc_parts(n, f[1], f[2])
+                run(fs)
+                run(las)
+                done.add(("hc", n))
+            elif k == "U":
+                fs, las = u_bank_parts(n, f[1])
+                run(fs)
+                run(las)
+            elif k == "W":
+                fs, la = words_parts(w_sb[:, n, :], w_grp, n, f[1], f[2] if len(f) > 2 else "zt")
+                run(fs)
+                la()
+            elif k == "Z":
+                fs, la = z_parts(n, f[1] if len(f) > 1 else "S", f[2] if len(f) > 2 else "zt")
+                run(fs)
+                la()
+                done.add(("z", n))
+            elif k == "p":
+                if n not in open_p:
+                    open_p[n] = p_parts(n)
+                    done.add(("p", n))
+                open_p[n][0]()
+                open_p[n] = open_p[n][1:]
+            elif k == "c":
+                plain_out(n)
+                done.add(("pp", n))
+            elif k == "w":
+                widen(n)
+                done.add(("w", n))
+            elif tok == "qW":
+                quantize(w_grp, w_q, w_s)
+            elif k == "q":
+                quant(n)
 
-        def turn_u(a):
-            fs, las = u_bank_parts(u_sb[:, a, :], u_t, a)
-            run(fs)
-            run(las)
-
-        def plain_round(s, groups):
-            ps = p_parts(s)
-            for n in range(4):
-                ps[n]()
-                if n < len(groups):
-                    fs, la = groups[n]()
-                    run(fs)
-                    la()
-            plain_out(s)
-            done.add(("p", s))
-            done.add(("pp", s))
-
-        def w_group(a):
-            return lambda: words_parts(w_sb[:, a, :], w_grp, a)
-
-        def z_group(x):
-            done.add(("z", x))
-            return lambda: z_parts(x)
-
-        for n in range(N_WARM):
-            idle_pass()
-        turn_hc(0, "hc", "V")
-        turn_hc(1, "mx", "V")
-        idle_pass()
-        for a in range(4):
-            turn_u(a)
-        idle_pass()
-        turn_hc(2, "mx", "V")
-        turn_hc(3, "hc", "V")
-        idle_pass()
-        widen(0)
-        plain_round(0, [w_group(0)])
-        widen(1)
-        plain_round(1, [w_group(1)])
-        widen(2)
-        plain_round(2, [w_group(2), w_group(3)])
-        widen(3)
-        quantize(w_grp, w_q, w_s)
-        plain_round(3, [z_group(0), z_group(1), z_group(2), z_group(3)])
-        widen(4)
-        turn_hc(4, "hc", "S")
-        fs, la = z_group(4)()
-        run(fs)
-        la()
-        quant(0)
-        turn_hc(5, "mx", "S")
-        turn_hc(6, "mx", "S")
-        widen(5)
-        turn_hc(7, "hc", "S")
-        fs, la = z_group(5)()
-        run(fs)
-        la()
-        widen(6)
-        widen(7)
+        for n in range(LW - 2):
+            if ("w", n) not in done:
+                widen(n)
+        for n in range(LH - 2):
+            if ("hc", n) not in done:
+                fs, las = hc_parts(n, "hc", "S")
+                run(fs)
+                run(las)
+                done.add(("hc", n))
+        for n in range(LZ - 2):
+            if ("z", n) not in done:
+                fs, la = z_parts(n)
+                run(fs)
+                la()
+                done.add(("z", n))
+        for n in range(LP - 2):
+            if ("p", n) not in done:
+                run(p_parts(n))
+                plain_out(n)
+                done.add(("p", n))
+                done.add(("pp", n))
 
         for s in range(-2, N_STEPS + GL + 1):
             for g in range(N_GROUPS):
@@ -397,10 +408,18 @@ def tile_treelstm_pa_kernel(tc, z_node_bytes, z_node_scale, z_children, W_f, U_f
                 gs = sum_parts(s - GL)
             ps = p_parts(s + LP) if 0 <= s + LP < N_STEPS and ("p", s + LP) not in done else []
             if WEAVE and len(ps) > 0:
+                if s - GL == 15:
+                    early, late = gs, []
+                    gs = []
+                elif s - GL == 16:
+                    early, late = [], gs
+                    gs = []
+                else:
+                    early, late = [], []
                 gaps = [
-                    zs[0:1] + hcs[0:2] + hcs[4:5] + gs[0:1],
+                    zs[0:1] + early + hcs[0:2] + hcs[4:5] + gs[0:1],
                     zs[1:2] + hcs[2:4] + hcs[5:6] + gs[1:2],
-                    zs[2:4] + gs[2:4],
+                    zs[2:4] + gs[2:4] + late,
                 ]
                 for n in range(4):
                     ps[n]()
@@ -410,8 +429,8 @@ def tile_treelstm_pa_kernel(tc, z_node_bytes, z_node_scale, z_children, W_f, U_f
             else:
                 for f in zs + hcs + gs + ps:
                     f()
-            for la in leaves:
-                la()
             if s == 15 + GL:
                 store_half(0)
+            for la in leaves:
+                la()
         store_half(1)

@@ -5,7 +5,7 @@ import concourse.mybir as mybir
 
 WEAVE = True
 HEAD_ORDER = """
-D D D D H0/hc/V H1/mx/V D U0/V U1/V D H2/mx/S H3/hc/S W0/S W1/S w0
+D D D D S0/V S1/V H0/hc/S H1/mx/S D U0/S U1/S w0 D H2/mx/S H3/hc/S W0/S W1/S
 w1 p0 p0 p0 p0 c0
 w2 w3 p1 Z0/S/mx p1 W2/S p1 W3/S p1 c1
 qW p2 Z1/S/mx p2 Z2 p2 Z3 p2 c2
@@ -38,7 +38,7 @@ GL = 3
 U_AT = -4
 W_AT = -4
 WQ_AT = -3
-HEAD = "c00 c01 U c02 c03 W0 scale z00 W1 z01 z02 z03 b c1 z1 z2 c2 z3 c3"
+HEAD = "scale c00 z00 c01 U c02 c03 W0 z01 W1 z02 z03 b c1 z1 z2 c2 z3 c3"
 Z_BUFS = 4
 C_BUFS = 4
 
@@ -65,6 +65,7 @@ def tile_treelstm_pa_kernel(tc, z_node_bytes, z_node_scale, z_children, W_f, U_f
         nc.scalar.activation(out=warm_out[:], in_=warm_in[:], func=ACT.Sigmoid)
 
         scale_bc = const.tile([P, SIZE], F32, name="scale_bc", tag="scale_bc")
+        scale_col = const.tile([P, SIZE // P], F32, name="scale_col", tag="scale_col")
         w_sb = const.tile([P, 4, SIZE], BF16, name="w_sb", tag="w_sb")
         u_sb = const.tile([P, 4, CH], BF16, name="u_sb", tag="u_sb")
         bias = const.tile([P, 4], BF16, name="bias", tag="bias")
@@ -276,7 +277,8 @@ def tile_treelstm_pa_kernel(tc, z_node_bytes, z_node_scale, z_children, W_f, U_f
         loaded = set()
         for tok in HEAD.split(" "):
             if tok == "scale":
-                nc.sync.dma_start(out=scale_bc[:], in_=z_node_scale.rearrange("a b k -> (a b k)").partition_broadcast(P))
+                with nc.allow_non_contiguous_dma(reason="the scales, k = 128 c + p on partition p: 8 single values to a partition"):
+                    nc.sync.dma_start(out=scale_col[:], in_=z_node_scale.rearrange("a b (c p) -> p (a b c)", p=P))
             elif tok.startswith("W"):
                 q = int(tok[1])
                 nc.sync.dma_start(
@@ -321,6 +323,11 @@ def tile_treelstm_pa_kernel(tc, z_node_bytes, z_node_scale, z_children, W_f, U_f
                 run(fs)
                 run(las)
                 done.add(("hc", n))
+            elif k == "S":
+                sb = psum.tile([P, 4, P], F32, name="zt", tag="zt")
+                for c in range(4):
+                    nc.tensor.transpose(sb[:, c, :], scale_col[:, 4 * n + c:4 * n + c + 1].to_broadcast([P, P]), ident_f[:])
+                move(f[1], scale_bc[:, 4 * P * n:4 * P * (n + 1)], sb[:].rearrange("p c j -> p (c j)"))
             elif k == "U":
                 fs, las = u_bank_parts(n, f[1])
                 run(fs)

@@ -195,7 +195,7 @@ def tile_treelstm_pa_kernel(tc, z_node_bytes, z_node_scale, z_children, W_f, U_f
             z_s[g] = work.tile([P, 2, GROUP], U8, name="z_s", tag="z_s", align_bytes=64)
             quantize(grp[g], z_q[g], z_s[g])
 
-        def p_parts(s):
+        def p_parts(s, split=False):
             g, a = divmod(s, 4)
             t = psum.tile([P, GROUP], F32, name="pl", tag="pl")
             pl_b[s] = t
@@ -203,6 +203,17 @@ def tile_treelstm_pa_kernel(tc, z_node_bytes, z_node_scale, z_children, W_f, U_f
             def one(kt):
                 return lambda: nc.tensor.matmul(t[:], lhsT=u_t[:, kt, P * a:P * (a + 1)], rhs=h_t[g][:, kt, :, :].rearrange("p j r -> p (j r)"), start=(kt == 0), stop=(kt == 3))
 
+            def half(c):
+                return lambda: nc.tensor.matmul(
+                    t[:, 256 * c:256 * (c + 1)],
+                    lhsT=u_t[:, 3, P * a:P * (a + 1)],
+                    rhs=h_t[g][:, 3, 2 * c:2 * c + 2, :].rearrange("p j r -> p (j r)"),
+                    start=False,
+                    stop=(c == 1),
+                )
+
+            if split:
+                return [one(kt) for kt in range(3)] + [half(0), half(1)]
             return [one(kt) for kt in range(4)]
 
         def mxmm(s):
@@ -413,7 +424,7 @@ def tile_treelstm_pa_kernel(tc, z_node_bytes, z_node_scale, z_children, W_f, U_f
                 leaves.append(la)
             if 0 <= s - GL < N_STEPS:
                 gs = sum_parts(s - GL)
-            ps = p_parts(s + LP) if 0 <= s + LP < N_STEPS and ("p", s + LP) not in done else []
+            ps = p_parts(s + LP, True) if 0 <= s + LP < N_STEPS and ("p", s + LP) not in done else []
             if WEAVE and len(ps) > 0:
                 if s - GL == 15:
                     early, late = gs, []
@@ -426,11 +437,12 @@ def tile_treelstm_pa_kernel(tc, z_node_bytes, z_node_scale, z_children, W_f, U_f
                 gaps = [
                     zs[0:1] + early + hcs[0:2] + hcs[4:5] + gs[0:1],
                     zs[1:2] + hcs[2:4] + hcs[5:6] + gs[1:2],
-                    zs[2:4] + gs[2:4] + late,
+                    zs[2:3] + gs[2:3],
+                    zs[3:4] + gs[3:4] + late,
                 ]
-                for n in range(4):
+                for n in range(5):
                     ps[n]()
-                    if n < 3:
+                    if n < 4:
                         for f in gaps[n]:
                             f()
             else:

@@ -8,9 +8,9 @@ HEAD_ORDER = """
 D D D D S0/V S1/V H0/hc/S H1/mx/S D U0/S U1/S w0 D H2/mx/S H3/hc/S W0/S W1/S
 w1 p0 p0 p0 p0 c0
 w2 w3 p1 Z0/S/mx p1 W2/S p1 W3/S p1 c1
-qW p2 Z1/S/mx p2 Z2 p2 Z3 p2 c2
-w4 q0 p3 H4/hc/S p3 H5/mx/S p3 p3 c3
-w5 w6 H6/mx/S Z4 H7/hc/S w7 Z5
+w4 w5 qW p2 Z1/S/mx p2 Z2 p2 Z3 p2 c2
+w6 q0 p3 H4/hc/S p3 H5/mx/S p3 p3 c3
+w7 H6/mx/S Z4 H7/hc/S Z5
 """
 
 F32 = mybir.dt.float32
@@ -34,7 +34,8 @@ LW = 10
 LZ = 8
 LP = 6
 LH = LP + 4
-GL = 3
+GL = 4
+ML = 2
 U_AT = -4
 W_AT = -4
 WQ_AT = -3
@@ -242,7 +243,7 @@ def tile_treelstm_pa_kernel(tc, z_node_bytes, z_node_scale, z_children, W_f, U_f
             x_t[s] = t
 
         def sig(s):
-            t = work.tile([P, GROUP], F32, name="f", tag="f", bufs=3)
+            t = work.tile([P, GROUP], F32, name="f", tag="f", bufs=ML + 2)
             nc.scalar.activation(out=t[:], in_=x_t[s][:], func=ACT.Sigmoid, bias=bias[:, s % 4:s % 4 + 1], scale=1.0)
             f_t[s] = t
 
@@ -404,8 +405,8 @@ def tile_treelstm_pa_kernel(tc, z_node_bytes, z_node_scale, z_children, W_f, U_f
                 sig(s)
             if 0 <= s + LW < N_STEPS:
                 widen(s + LW)
-            if 0 <= s - 1 < N_STEPS:
-                mul(s - 1)
+            if 0 <= s - ML < N_STEPS:
+                mul(s - ML)
             if (s + 3) % 4 == 0 and 0 <= (s + 3) // 4 < N_GROUPS:
                 quant((s + 3) // 4)
             if 0 <= s + LP - 1 < N_STEPS and ("pp", s + LP - 1) not in done:

@@ -39,7 +39,7 @@ ML = 2
 U_AT = -4
 W_AT = -4
 WQ_AT = -3
-HEAD = "scale c00 z00 c01 U c02 c03 W0 z01 W1 z02 z03 b c1 z1 z2 c2 z3 c3"
+HEAD = "scale c00 z00 c01 U c02 c03 W0 z01 W1 z02 z03 z1 c1 z2 c2 b z3 c3"
 Z_BUFS = 4
 C_BUFS = 4
 
@@ -238,7 +238,7 @@ def tile_treelstm_pa_kernel(tc, z_node_bytes, z_node_scale, z_children, W_f, U_f
             pp_t[s] = t
 
         def add(s):
-            t = work.tile([P, GROUP], F32, name="x", tag="x")
+            t = work.tile([P, GROUP], F32, name="x", tag="x", bufs=ML + 1)
             nc.vector.tensor_tensor(out=t[:], in0=mx_b[s][:], in1=pp_t[s][:], op=ALU.add)
             x_t[s] = t
 
@@ -289,8 +289,7 @@ def tile_treelstm_pa_kernel(tc, z_node_bytes, z_node_scale, z_children, W_f, U_f
         loaded = set()
         for tok in HEAD.split(" "):
             if tok == "scale":
-                with nc.allow_non_contiguous_dma(reason="the scales, k = 128 c + p on partition p: 8 single values to a partition"):
-                    nc.sync.dma_start(out=scale_col[:], in_=z_node_scale.rearrange("a b (c p) -> p (a b c)", p=P))
+                nc.sync.dma_start(out=scale_col[:], in_=z_node_scale.rearrange("a b (p c) -> p (a b c)", p=P))
             elif tok.startswith("W"):
                 q = int(tok[1])
                 nc.sync.dma_start(
@@ -339,7 +338,7 @@ def tile_treelstm_pa_kernel(tc, z_node_bytes, z_node_scale, z_children, W_f, U_f
                 sb = psum.tile([P, 4, P], F32, name="zt", tag="zt")
                 for c in range(4):
                     nc.tensor.transpose(sb[:, c, :], scale_col[:, 4 * n + c:4 * n + c + 1].to_broadcast([P, P]), ident_f[:])
-                move(f[1], scale_bc[:, 4 * P * n:4 * P * (n + 1)], sb[:].rearrange("p c j -> p (c j)"))
+                move(f[1], scale_bc[:].rearrange("p (j c) -> p j c", c=8)[:, :, 4 * n:4 * n + 4], sb[:].rearrange("p c j -> p j c"))
             elif k == "U":
                 fs, las = u_bank_parts(n, f[1])
                 run(fs)

@@ -35,12 +35,23 @@ LZ = 8
 LP = 6
 LH = LP + 4
 GL = 4
+GT = 4
 ML = 2
 U_AT = -4
 W_AT = -4
 WQ_AT = -3
 HEAD = "scale c00 z00 c01 U c02 c03 W0 z01 W1 z02 z03 z1 c1 z2 c2 b z3 c3"
 Z_BUFS = 4
+HOLD = 22
+ZB = 6
+K0 = 16
+G_FROM = 26
+G_MANY = 3
+G_BUFS = 14
+Z_TWO = 22
+Q7 = 25
+M_TO = {22: 25, 23: 26, 24: 27, 25: 27, 26: 29, 27: 31}
+MX_TAG = {25: "hc", 27: "acc", 29: "hc", 31: "acc"}
 C_BUFS = 4
 
 
@@ -122,7 +133,7 @@ def tile_treelstm_pa_kernel(tc, z_node_bytes, z_node_scale, z_children, W_f, U_f
 
         def widen(x):
             g, j = divmod(x, 4)
-            t = work.tile([P, SIZE], BF16, name="zb", tag="zb", bufs=LW - LZ + 4)
+            t = work.tile([P, SIZE], BF16, name="zb", tag="zb", bufs=ZB)
             nc.vector.tensor_tensor(out=t[:], in0=zby[g][:, j, :].bitcast(FP8), in1=scale_bc[:], op=ALU.mult)
             zbt[x] = t
 
@@ -219,7 +230,8 @@ def tile_treelstm_pa_kernel(tc, z_node_bytes, z_node_scale, z_children, W_f, U_f
 
         def mxmm(s):
             g, a = divmod(s, 4)
-            t = psum.tile([P, GROUP], F32, name="mx", tag="mx")
+            tag = MX_TAG.get(s, "mx")
+            t = psum.tile([P, GROUP], F32, name=tag, tag=tag, bufs=1 if tag in ("hc", "acc") else 2)
             for c in range(2):
                 nc.tensor.matmul_mx(
                     out=t[:],
@@ -250,7 +262,7 @@ def tile_treelstm_pa_kernel(tc, z_node_bytes, z_node_scale, z_children, W_f, U_f
         def mul(s):
             g, a = divmod(s, 4)
             q, e = divmod(a, 2)
-            t = work.tile([P, GROUP], F32, name="gm", tag="gm", bufs=GL + 2)
+            t = work.tile([P, GROUP], F32, name="gm", tag="gm", bufs=G_BUFS)
             cells = h_t[g][:, 4 + 2 * q:6 + 2 * q, :, :].rearrange("p h j (r e) -> p j h r e", e=2)[:, :, :, :, e]
             nc.vector.tensor_tensor(
                 out=t[:].rearrange("p (j h r) -> p j h r", j=4, h=2),
@@ -263,28 +275,40 @@ def tile_treelstm_pa_kernel(tc, z_node_bytes, z_node_scale, z_children, W_f, U_f
         def sum_parts(s):
             g, a = divmod(s, 4)
             hb = g // 4
-            if s % 16 == 0:
-                acc[hb] = psum.tile([P, 4, P], F32, name="acc", tag="acc", bufs=1)
+            q, e = divmod(a, 2)
+            if hb == 0:
+                if s == 0:
+                    acc[hb] = psum.tile([P, 4, P], F32, name="acc", tag="acc", bufs=1)
+                into, first, last = acc[hb][:, a, :], s == 0, s == 15
+            else:
+                if s in (16, 18):
+                    acc[hb, q] = psum.tile([P, 2, P], F32, name="zt", tag="zt")
+                into, first, last = acc[hb, q][:, e, :], s in (16, 18), s in (29, 31)
 
             def one(j):
                 return lambda: nc.tensor.matmul(
-                    acc[hb][:, a, :],
+                    into,
                     lhsT=g_t[s][:, P * j:P * (j + 1)],
                     rhs=ident_f[:],
                     is_transpose=True,
-                    start=(s % 16 == 0 and j == 0),
-                    stop=(s % 16 == 15 and j == 3),
+                    start=(first and j == 0),
+                    stop=(last and j == 3),
                 )
 
             return [one(j) for j in range(4)]
 
-        def store_half(hb):
+        def store_half():
             osb = work.tile([P, CH], F32, name="osb", tag="osb")
             nc.scalar.copy(
                 out=osb[:].rearrange("p (q w e) -> p q w e", q=2, e=2),
-                in_=acc[hb][:].rearrange("p (q e) w -> p q w e", q=2),
+                in_=acc[0][:].rearrange("p (q e) w -> p q w e", q=2),
             )
-            nc.sync.dma_start(out=out[P * hb:P * (hb + 1), :], in_=osb[:])
+            nc.sync.dma_start(out=out[0:P, :], in_=osb[:])
+
+        def store_quarter(q):
+            osq = work.tile([P, CH // 2], F32, name="osq", tag="osq")
+            nc.scalar.copy(out=osq[:].rearrange("p (w e) -> p w e", e=2), in_=acc[1, q][:].rearrange("p e w -> p w e"))
+            nc.sync.dma_start(out=out[P:2 * P, CH // 2 * q:CH // 2 * (q + 1)], in_=osq[:])
 
         loaded = set()
         for tok in HEAD.split(" "):
@@ -391,6 +415,10 @@ def tile_treelstm_pa_kernel(tc, z_node_bytes, z_node_scale, z_children, W_f, U_f
                 done.add(("p", n))
                 done.add(("pp", n))
 
+        m_done = -1
+        g_done = -1
+        stored = False
+        held = []
         for s in range(-2, N_STEPS + GL + 1):
             for g in range(N_GROUPS):
                 if "z" + str(g) not in loaded and s >= 4 * (g - Z_BUFS) + 4 - LW:
@@ -402,16 +430,20 @@ def tile_treelstm_pa_kernel(tc, z_node_bytes, z_node_scale, z_children, W_f, U_f
             if 0 <= s < N_STEPS:
                 add(s)
                 sig(s)
+            for la in held:
+                la()
+            held = []
             if 0 <= s + LW < N_STEPS:
                 widen(s + LW)
             if 0 <= s - ML < N_STEPS:
                 mul(s - ML)
-            if (s + 3) % 4 == 0 and 0 <= (s + 3) // 4 < N_GROUPS:
-                quant((s + 3) // 4)
+            if (s + 3) % 4 == 0 and 0 <= (s + 3) // 4 < N_GROUPS - 1 or s == Q7:
+                quant((s + 3) // 4 if s != Q7 else N_GROUPS - 1)
             if 0 <= s + LP - 1 < N_STEPS and ("pp", s + LP - 1) not in done:
                 plain_out(s + LP - 1)
-            if 0 <= s + 2 < N_STEPS:
-                mxmm(s + 2)
+            while m_done < min(M_TO.get(s, s + 2), N_STEPS - 1):
+                m_done += 1
+                mxmm(m_done)
             zs = []
             hcs = []
             gs = []
@@ -422,8 +454,20 @@ def tile_treelstm_pa_kernel(tc, z_node_bytes, z_node_scale, z_children, W_f, U_f
             if 0 <= s + LZ < N_STEPS and ("z", s + LZ) not in done:
                 zs, la = z_parts(s + LZ)
                 leaves.append(la)
-            if 0 <= s - GL < N_STEPS:
+                done.add(("z", s + LZ))
+                if s == Z_TWO:
+                    zs2, la = z_parts(s + LZ + 1)
+                    zs = [zs[0], zs[1], zs[2], zs[3]] + zs2
+                    leaves.append(la)
+                    done.add(("z", s + LZ + 1))
+            if 0 <= s - GL < K0:
                 gs = sum_parts(s - GL)
+                g_done = s - GL
+            elif s >= G_FROM:
+                for n in range(G_MANY):
+                    if g_done + 1 <= min(s - (GT if s < N_STEPS else ML), N_STEPS - 1):
+                        g_done += 1
+                        gs = gs + sum_parts(g_done)
             ps = p_parts(s + LP, True) if 0 <= s + LP < N_STEPS and ("p", s + LP) not in done else []
             if WEAVE and len(ps) > 0:
                 if s - GL == 15:
@@ -440,16 +484,26 @@ def tile_treelstm_pa_kernel(tc, z_node_bytes, z_node_scale, z_children, W_f, U_f
                     zs[2:3] + gs[2:3],
                     zs[3:4] + gs[3:4] + late,
                 ]
+                for n in range(4, len(zs)):
+                    gaps[n - 4].append(zs[n])
                 for n in range(5):
                     ps[n]()
                     if n < 4:
                         for f in gaps[n]:
                             f()
             else:
+                if s == 15 + GL:
+                    pass
                 for f in zs + hcs + gs + ps:
                     f()
             if s == 15 + GL:
-                store_half(0)
+                store_half()
+            if s >= HOLD:
+                held = leaves
+                leaves = []
             for la in leaves:
                 la()
-        store_half(1)
+            if g_done >= 29 and not stored:
+                store_quarter(0)
+                stored = True
+        store_quarter(1)

@@ -5,12 +5,12 @@ import concourse.mybir as mybir
 
 WEAVE = True
 HEAD_ORDER = """
-D D D D S0/V S1/V H0/hc/S H1/mx/S D U0/S U1/S w0 D H2/mx/S H3/hc/S W0/S W1/S
+D D S0/V S1/S D D H0/hc/S H1/mx/S D U0/S U1/S w0 D H2/mx/S H3/hc/S W0/S W1/S
 w1 p0 p0 p0 p0 c0
 w2 w3 p1 Z0/S/mx p1 W2/S p1 W3/S p1 c1
-w4 w5 qW p2 Z1/S/mx p2 Z2 p2 Z3 p2 c2
-w6 q0 p3 H4/hc/S p3 H5/mx/S p3 p3 c3
-w7 H6/mx/S Z4 H7/hc/S Z5
+w4 w5 w6 qW p2 Z1/S/mx p2 Z2 p2 Z3 p2 c2
+w7 q0 p3 H4/hc/S p3 H5/mx/S p3 p3 c3
+H6/mx/S Z4 H7/hc/S Z5
 """
 
 F32 = mybir.dt.float32
@@ -40,14 +40,14 @@ ML = 2
 U_AT = -4
 W_AT = -4
 WQ_AT = -3
-HEAD = "scale c00 z00 c01 U c02 c03 W0 z01 W1 z02 z03 z1 c1 z2 c2 b z3 c3"
+HEAD = "scale c00 z00 c01 U c02 z01 c03 W0 z02 W1 z03 z1 c1 z2 c2 b z3 c3"
 Z_BUFS = 4
 HOLD = 22
-ZB = 6
+ZB = 8
 K0 = 16
 G_FROM = 26
 G_MANY = 3
-G_BUFS = 14
+G_BUFS = 13
 Z_TWO = 22
 Q7 = 25
 M_TO = {22: 25, 23: 26, 24: 27, 25: 27, 26: 29, 27: 31}

@@ -134,7 +134,7 @@ def tile_treelstm_pa_kernel(tc, z_node_bytes, z_node_scale, z_children, W_f, U_f
         def widen(x):
             g, j = divmod(x, 4)
             t = work.tile([P, SIZE], BF16, name="zb", tag="zb", bufs=ZB)
-            nc.vector.tensor_tensor(out=t[:], in0=zby[g][:, j, :].bitcast(FP8), in1=scale_bc[:], op=ALU.mult)
+            nc.vector.tensor_tensor(out=t[:], in0=scale_bc[:], in1=zby[g][:, j, :].bitcast(FP8), op=ALU.mult)
             zbt[x] = t
 
         def words_parts(src, dst, col, eng="S", tag="zt"):

from contextlib import ExitStack

import concourse.masks as masks
import concourse.mybir as mybir

WEAVE = True
HEAD_ORDER = """
D D S0/V S1/S D D H0/hc/S H1/mx/S D U0/S U1/S w0 D H2/mx/S H3/hc/S W0/S W1/S
w1 p0 p0 p0 p0 c0
w2 w3 p1 Z0/S/mx p1 W2/S p1 W3/S p1 c1
w4 w5 w6 qW p2 Z1/S/mx p2 Z2 p2 Z3 p2 c2
w7 q0 p3 H4/hc/S p3 H5/mx/S p3 p3 c3
H6/mx/S Z4 H7/hc/S Z5
"""

F32 = mybir.dt.float32
BF16 = mybir.dt.bfloat16
U32 = mybir.dt.uint32
U8 = mybir.dt.uint8
FP8 = mybir.dt.float8_e4m3fn
FP8X4 = mybir.dt.float8_e4m3fn_x4
ALU = mybir.AluOpType
ACT = mybir.ActivationFunctionType

P = 128
NODES, KIDS, SIZE, CH = 256, 16, 1024, 512
TOKENS = NODES * KIDS
FLOPS = 2 * TOKENS * CH * (SIZE + CH)

GROUP = 512
N_GROUPS = TOKENS // GROUP
N_STEPS = 4 * N_GROUPS
LW = 10
LZ = 8
LP = 6
LH = LP + 4
GL = 4
GT = 4
ML = 2
U_AT = -4
W_AT = -4
WQ_AT = -3
HEAD = "scale c00 z00 c01 U c02 z01 c03 W0 z02 W1 z03 z1 c1 z2 c2 b z3 c3"
Z_BUFS = 4
HOLD = 22
ZB = 8
K0 = 16
G_FROM = 26
G_MANY = 3
G_BUFS = 13
Z_TWO = 22
Q7 = 25
M_TO = {22: 25, 23: 26, 24: 27, 25: 27, 26: 29, 27: 31}
MX_TAG = {25: "hc", 27: "acc", 29: "hc", 31: "acc"}
C_BUFS = 4


def tile_treelstm_pa_kernel(tc, z_node_bytes, z_node_scale, z_children, W_f, U_f, b_f, out):
    nc = tc.nc

    with ExitStack() as ctx:
        const = ctx.enter_context(tc.tile_pool(name="const", bufs=1))
        loads = ctx.enter_context(tc.tile_pool(name="loads", bufs=4))
        work = ctx.enter_context(tc.tile_pool(name="work", bufs=2))
        psum = ctx.enter_context(tc.psum_pool(name="psum", bufs=2))

        ctx.enter_context(tc.manual_schedule())
        ident_f = const.tile([P, P], F32, name="ident_f", tag="ident_f")
        masks.make_identity(nc, ident_f[:])
        ident_b = const.tile([P, P], BF16, name="ident_b", tag="ident_b")
        masks.make_identity(nc, ident_b[:])
        warm_in = const.tile([P, 1], F32, name="warm_in", tag="warm_in")
        warm_out = const.tile([P, 1], F32, name="warm_out", tag="warm_out")
        idle_in = const.tile([P, GROUP], BF16, name="idle_in", tag="idle_in")
        nc.vector.memset(idle_in[:], 0.0)
        nc.vector.memset(warm_in[:], 0.0)
        nc.scalar.activation(out=warm_out[:], in_=warm_in[:], func=ACT.Sigmoid)

        scale_bc = const.tile([P, SIZE], F32, name="scale_bc", tag="scale_bc")
        scale_col = const.tile([P, SIZE // P], F32, name="scale_col", tag="scale_col")
        w_sb = const.tile([P, 4, SIZE], BF16, name="w_sb", tag="w_sb")
        u_sb = const.tile([P, 4, CH], BF16, name="u_sb", tag="u_sb")
        bias = const.tile([P, 4], BF16, name="bias", tag="bias")
        w_grp = const.tile([P, 2, CH, 4], BF16, name="w_grp", tag="w_grp", align_bytes=64)
        w_q = const.tile([P, 2, CH], U32, name="w_q", tag="w_q", align_bytes=64)
        w_s = const.tile([P, 2, CH], U8, name="w_s", tag="w_s", align_bytes=64)
        u_t = const.tile([P, 4, CH], BF16, name="u_t", tag="u_t")


        zby = {}
        chd = {}
        zbt = {}
        grp = {}
        h_t = {}
        c_t = {}
        z_q = {}
        z_s = {}
        pl_b = {}
        mx_b = {}
        pp_t = {}
        x_t = {}
        f_t = {}
        g_t = {}
        acc = {}

        def load_rows(src3, t, g, piece):
            hb, gam = divmod(g, 4)
            src = src3[P * hb:P * (hb + 1), 4 * gam:4 * (gam + 1), :]
            if piece is None:
                nc.sync.dma_start(out=t[:], in_=src)
            else:
                nc.sync.dma_start(out=t[:, piece, :], in_=src[:, piece, :])

        def load_bytes(g, piece):
            if g not in zby:
                zby[g] = loads.tile([P, 4, SIZE], U8, name="zbytes", tag="zbytes", bufs=Z_BUFS)
            load_rows(z_node_bytes, zby[g], g, piece)

        def load_children(g, piece):
            if g not in chd:
                chd[g] = loads.tile([P, 4, SIZE], BF16, name="child", tag="child", bufs=C_BUFS)
            load_rows(z_children, chd[g], g, piece)

        def move(eng, out, in_):
            if eng == "V":
                nc.vector.tensor_copy(out=out, in_=in_)
            else:
                nc.scalar.copy(out=out, in_=in_)

        def idle_pass():
            t = psum.tile([P, GROUP], F32, name="pl", tag="pl")
            nc.tensor.matmul(t[:], lhsT=idle_in[:, 0:P], rhs=idle_in[:], start=True, stop=True)

        def widen(x):
            g, j = divmod(x, 4)
            t = work.tile([P, SIZE], BF16, name="zb", tag="zb", bufs=ZB)
            nc.vector.tensor_tensor(out=t[:], in0=scale_bc[:], in1=zby[g][:, j, :].bitcast(FP8), op=ALU.mult)
            zbt[x] = t

        def words_parts(src, dst, col, eng="S", tag="zt"):
            zt = psum.tile([P, 2, 2, P], F32, name=tag, tag=tag, bufs=(1 if tag in ("hc", "acc") else 2))
            words = src.bitcast(F32)

            def one(g, u):
                return lambda: nc.tensor.transpose(zt[:, g, u, :], words[:, 256 * g + u:256 * (g + 1):2], ident_f[:])

            def leave():
                dst_words = dst[:].rearrange("p g t k -> p (g t k)").bitcast(F32).rearrange("p (g t u) -> p g t u", g=2, u=2)
                move(eng, dst_words[:, :, P * col:P * (col + 1), :], zt[:].rearrange("p g u r -> p g r u"))

            return [one(g, u) for g in range(2) for u in range(2)], leave

        def u_bank_parts(pair, eng):
            ub = psum.tile([P, 512], F32, name="zt", tag="zt")
            uv = ub[:].bitcast(BF16).rearrange("p (a kt m) -> p a kt m", a=2, kt=4)

            def one(a, kt):
                return lambda: nc.tensor.transpose(uv[:, a, kt, :], u_sb[:, 2 * pair + a, P * kt:P * (kt + 1)], ident_b[:])

            def leave():
                move(
                    eng,
                    u_t[:, :, 2 * P * pair:2 * P * (pair + 1)].rearrange("p kt (a m) -> p kt a m", a=2),
                    uv.rearrange("p a kt m -> p kt a m"),
                )

            return [one(a, kt) for a in range(2) for kt in range(4)], [leave]

        def hc_bank_parts(h_src, c_src, dst, col, tag, eng):
            hc = psum.tile([P, 512], F32, name=tag, tag=tag, bufs=(1 if tag == "hc" else 2))
            hv = hc[:, 0:256].bitcast(BF16).rearrange("p (kt r) -> p kt r", kt=4)
            words = c_src.bitcast(F32)

            def one_h(kt):
                return lambda: nc.tensor.transpose(hv[:, kt, :], h_src[:, P * kt:P * (kt + 1)], ident_b[:])

            def one_c(q):
                return lambda: nc.tensor.transpose(hc[:, 256 + P * q:256 + P * (q + 1)], words[:, P * q:P * (q + 1)], ident_f[:])

            def leave():
                dst_words = dst[:].rearrange("p i j r -> p (i j r)").bitcast(F32).rearrange("p (i j w) -> p i j w", i=8, j=4)
                move(eng, dst_words[:, :, col, :], hc[:].rearrange("p (i w) -> p i w", i=8))

            return [one_h(kt) for kt in range(4)] + [one_c(q) for q in range(2)], [leave]

        def z_parts(x, eng="S", tag="zt"):
            g, j = divmod(x, 4)
            if j == 0:
                grp[g] = work.tile([P, 2, GROUP, 4], BF16, name="grp", tag="grp", align_bytes=64)
            return words_parts(zbt[x][:], grp[g], j, eng, tag)

        def hc_parts(x, tag="hc", eng="S"):
            g, j = divmod(x, 4)
            if j == 0:
                h_t[g] = work.tile([P, 8, 4, P], BF16, name="hc_t", tag="hc_t", bufs=(LH + 7) // 4 + 2)
            return hc_bank_parts(chd[g][:, j, 0:CH], chd[g][:, j, CH:SIZE], h_t[g], j, tag, eng)

        def quantize(src, codes, scales):
            nc.vector.quantize_mx(
                out=codes[:].rearrange("p g t -> p (g t)").bitcast(FP8X4),
                scales=scales[:].rearrange("p g t -> p (g t)"),
                in_=src[:].rearrange("p g t k -> p (g t k)"),
            )

        def quant(g):
            z_q[g] = work.tile([P, 2, GROUP], U32, name="z_q", tag="z_q", align_bytes=64)
            z_s[g] = work.tile([P, 2, GROUP], U8, name="z_s", tag="z_s", align_bytes=64)
            quantize(grp[g], z_q[g], z_s[g])

        def p_parts(s, split=False):
            g, a = divmod(s, 4)
            t = psum.tile([P, GROUP], F32, name="pl", tag="pl")
            pl_b[s] = t

            def one(kt):
                return lambda: nc.tensor.matmul(t[:], lhsT=u_t[:, kt, P * a:P * (a + 1)], rhs=h_t[g][:, kt, :, :].rearrange("p j r -> p (j r)"), start=(kt == 0), stop=(kt == 3))

            def half(c):
                return lambda: nc.tensor.matmul(
                    t[:, 256 * c:256 * (c + 1)],
                    lhsT=u_t[:, 3, P * a:P * (a + 1)],
                    rhs=h_t[g][:, 3, 2 * c:2 * c + 2, :].rearrange("p j r -> p (j r)"),
                    start=False,
                    stop=(c == 1),
                )

            if split:
                return [one(kt) for kt in range(3)] + [half(0), half(1)]
            return [one(kt) for kt in range(4)]

        def mxmm(s):
            g, a = divmod(s, 4)
            tag = MX_TAG.get(s, "mx")
            t = psum.tile([P, GROUP], F32, name=tag, tag=tag, bufs=1 if tag in ("hc", "acc") else 2)
            for c in range(2):
                nc.tensor.matmul_mx(
                    out=t[:],
                    lhsT=w_q[:, c, P * a:P * (a + 1)].bitcast(FP8X4),
                    lhsT_scale=w_s[:, c, P * a:P * (a + 1)],
                    rhs=z_q[g][:, c, :].bitcast(FP8X4),
                    rhs_scale=z_s[g][:, c, :],
                    start=(c == 0),
                    stop=(c == 1),
                )
            mx_b[s] = t

        def plain_out(s):
            t = work.tile([P, GROUP], F32, name="pp", tag="pp", bufs=LP + 2)
            nc.scalar.copy(out=t[:], in_=pl_b[s][:])
            pp_t[s] = t

        def add(s):
            t = work.tile([P, GROUP], F32, name="x", tag="x", bufs=ML + 1)
            nc.vector.tensor_tensor(out=t[:], in0=mx_b[s][:], in1=pp_t[s][:], op=ALU.add)
            x_t[s] = t

        def sig(s):
            t = work.tile([P, GROUP], F32, name="f", tag="f", bufs=ML + 2)
            nc.scalar.activation(out=t[:], in_=x_t[s][:], func=ACT.Sigmoid, bias=bias[:, s % 4:s % 4 + 1], scale=1.0)
            f_t[s] = t

        def mul(s):
            g, a = divmod(s, 4)
            q, e = divmod(a, 2)
            t = work.tile([P, GROUP], F32, name="gm", tag="gm", bufs=G_BUFS)
            cells = h_t[g][:, 4 + 2 * q:6 + 2 * q, :, :].rearrange("p h j (r e) -> p j h r e", e=2)[:, :, :, :, e]
            nc.vector.tensor_tensor(
                out=t[:].rearrange("p (j h r) -> p j h r", j=4, h=2),
                in0=f_t[s][:].rearrange("p (j h r) -> p j h r", j=4, h=2),
                in1=cells,
                op=ALU.mult,
            )
            g_t[s] = t

        def sum_parts(s):
            g, a = divmod(s, 4)
            hb = g // 4
            q, e = divmod(a, 2)
            if hb == 0:
                if s == 0:
                    acc[hb] = psum.tile([P, 4, P], F32, name="acc", tag="acc", bufs=1)
                into, first, last = acc[hb][:, a, :], s == 0, s == 15
            else:
                if s in (16, 18):
                    acc[hb, q] = psum.tile([P, 2, P], F32, name="zt", tag="zt")
                into, first, last = acc[hb, q][:, e, :], s in (16, 18), s in (29, 31)

            def one(j):
                return lambda: nc.tensor.matmul(
                    into,
                    lhsT=g_t[s][:, P * j:P * (j + 1)],
                    rhs=ident_f[:],
                    is_transpose=True,
                    start=(first and j == 0),
                    stop=(last and j == 3),
                )

            return [one(j) for j in range(4)]

        def store_half():
            osb = work.tile([P, CH], F32, name="osb", tag="osb")
            nc.scalar.copy(
                out=osb[:].rearrange("p (q w e) -> p q w e", q=2, e=2),
                in_=acc[0][:].rearrange("p (q e) w -> p q w e", q=2),
            )
            nc.sync.dma_start(out=out[0:P, :], in_=osb[:])

        def store_quarter(q):
            osq = work.tile([P, CH // 2], F32, name="osq", tag="osq")
            nc.scalar.copy(out=osq[:].rearrange("p (w e) -> p w e", e=2), in_=acc[1, q][:].rearrange("p e w -> p w e"))
            nc.sync.dma_start(out=out[P:2 * P, CH // 2 * q:CH // 2 * (q + 1)], in_=osq[:])

        loaded = set()
        for tok in HEAD.split(" "):
            if tok == "scale":
                nc.sync.dma_start(out=scale_col[:], in_=z_node_scale.rearrange("a b (p c) -> p (a b c)", p=P))
            elif tok.startswith("W"):
                q = int(tok[1])
                nc.sync.dma_start(
                    out=w_sb[:, 2 * q:2 * q + 2, :].rearrange("m e k -> m (e k)"),
                    in_=W_f.rearrange("(q m e) k -> q m (e k)", q=2, m=P, e=2)[q],
                )
            elif tok == "U":
                nc.sync.dma_start(
                    out=u_sb[:].rearrange("m (q e) k -> m q (e k)", q=2),
                    in_=U_f.rearrange("(q m e) k -> m q (e k)", q=2, m=P, e=2),
                )
            elif tok == "b":
                with nc.allow_non_contiguous_dma(reason="the bias, two neighbouring channels to a partition"):
                    nc.sync.dma_start(
                        out=bias[:].rearrange("m (q e) -> m q e", q=2),
                        in_=b_f.rearrange("(q m e) -> m q e", q=2, m=P, e=2),
                    )
            elif tok.startswith("z"):
                load_bytes(int(tok[1]), int(tok[2]) if len(tok) > 2 else None)
                loaded.add(tok[0:2])
            else:
                load_children(int(tok[1]), int(tok[2]) if len(tok) > 2 else None)
                loaded.add(tok[0:2])

        done = set()

        def run(parts):
            for f in parts:
                f()

        open_p = {}
        for tok in HEAD_ORDER.split():
            f = tok.split("/")
            k = f[0][0]
            n = int(f[0][1:]) if len(f[0]) > 1 and f[0][1:] != "W" else 0
            if (k == "H" and n >= LH - 2) or (k == "Z" and n >= LZ - 2) or (k in ("p", "c") and n >= LP - 2) or (k == "w" and n >= LW - 2):
                continue
            if tok == "D":
                idle_pass()
            elif k == "H":
                fs, las = hc_parts(n, f[1], f[2])
                run(fs)
                run(las)
                done.add(("hc", n))
            elif k == "S":
                sb = psum.tile([P, 4, P], F32, name="zt", tag="zt")
                for c in range(4):
                    nc.tensor.transpose(sb[:, c, :], scale_col[:, 4 * n + c:4 * n + c + 1].to_broadcast([P, P]), ident_f[:])
                move(f[1], scale_bc[:].rearrange("p (j c) -> p j c", c=8)[:, :, 4 * n:4 * n + 4], sb[:].rearrange("p c j -> p j c"))
            elif k == "U":
                fs, las = u_bank_parts(n, f[1])
                run(fs)
                run(las)
            elif k == "W":
                fs, la = words_parts(w_sb[:, n, :], w_grp, n, f[1], f[2] if len(f) > 2 else "zt")
                run(fs)
                la()
            elif k == "Z":
                fs, la = z_parts(n, f[1] if len(f) > 1 else "S", f[2] if len(f) > 2 else "zt")
                run(fs)
                la()
                done.add(("z", n))
            elif k == "p":
                if n not in open_p:
                    open_p[n] = p_parts(n)
                    done.add(("p", n))
                open_p[n][0]()
                open_p[n] = open_p[n][1:]
            elif k == "c":
                plain_out(n)
                done.add(("pp", n))
            elif k == "w":
                widen(n)
                done.add(("w", n))
            elif tok == "qW":
                quantize(w_grp, w_q, w_s)
            elif k == "q":
                quant(n)

        for n in range(LW - 2):
            if ("w", n) not in done:
                widen(n)
        for n in range(LH - 2):
            if ("hc", n) not in done:
                fs, las = hc_parts(n, "hc", "S")
                run(fs)
                run(las)
                done.add(("hc", n))
        for n in range(LZ - 2):
            if ("z", n) not in done:
                fs, la = z_parts(n)
                run(fs)
                la()
                done.add(("z", n))
        for n in range(LP - 2):
            if ("p", n) not in done:
                run(p_parts(n))
                plain_out(n)
                done.add(("p", n))
                done.add(("pp", n))

        m_done = -1
        g_done = -1
        stored = False
        held = []
        for s in range(-2, N_STEPS + GL + 1):
            for g in range(N_GROUPS):
                if "z" + str(g) not in loaded and s >= 4 * (g - Z_BUFS) + 4 - LW:
                    load_bytes(g, None)
                    loaded.add("z" + str(g))
                if "c" + str(g) not in loaded and s >= 4 * (g - C_BUFS) + 4 - LH:
                    load_children(g, None)
                    loaded.add("c" + str(g))
            if 0 <= s < N_STEPS:
                add(s)
                sig(s)
            for la in held:
                la()
            held = []
            if 0 <= s + LW < N_STEPS:
                widen(s + LW)
            if 0 <= s - ML < N_STEPS:
                mul(s - ML)
            if (s + 3) % 4 == 0 and 0 <= (s + 3) // 4 < N_GROUPS - 1 or s == Q7:
                quant((s + 3) // 4 if s != Q7 else N_GROUPS - 1)
            if 0 <= s + LP - 1 < N_STEPS and ("pp", s + LP - 1) not in done:
                plain_out(s + LP - 1)
            while m_done < min(M_TO.get(s, s + 2), N_STEPS - 1):
                m_done += 1
                mxmm(m_done)
            zs = []
            hcs = []
            gs = []
            leaves = []
            if 0 <= s + LH < N_STEPS and ("hc", s + LH) not in done:
                hcs, las = hc_parts(s + LH)
                leaves.extend(las)
            if 0 <= s + LZ < N_STEPS and ("z", s + LZ) not in done:
                zs, la = z_parts(s + LZ)
                leaves.append(la)
                done.add(("z", s + LZ))
                if s == Z_TWO:
                    zs2, la = z_parts(s + LZ + 1)
                    zs = [zs[0], zs[1], zs[2], zs[3]] + zs2
                    leaves.append(la)
                    done.add(("z", s + LZ + 1))
            if 0 <= s - GL < K0:
                gs = sum_parts(s - GL)
                g_done = s - GL
            elif s >= G_FROM:
                for n in range(G_MANY):
                    if g_done + 1 <= min(s - (GT if s < N_STEPS else ML), N_STEPS - 1):
                        g_done += 1
                        gs = gs + sum_parts(g_done)
            ps = p_parts(s + LP, True) if 0 <= s + LP < N_STEPS and ("p", s + LP) not in done else []
            if WEAVE and len(ps) > 0:
                if s - GL == 15:
                    early, late = gs, []
                    gs = []
                elif s - GL == 16:
                    early, late = [], gs
                    gs = []
                else:
                    early, late = [], []
                gaps = [
                    zs[0:1] + early + hcs[0:2] + hcs[4:5] + gs[0:1],
                    zs[1:2] + hcs[2:4] + hcs[5:6] + gs[1:2],
                    zs[2:3] + gs[2:3],
                    zs[3:4] + gs[3:4] + late,
                ]
                for n in range(4, len(zs)):
                    gaps[n - 4].append(zs[n])
                for n in range(5):
                    ps[n]()
                    if n < 4:
                        for f in gaps[n]:
                            f()
            else:
                if s == 15 + GL:
                    pass
                for f in zs + hcs + gs + ps:
                    f()
            if s == 15 + GL:
                store_half()
            if s >= HOLD:
                held = leaves
                leaves = []
            for la in leaves:
                la()
            if g_done >= 29 and not stored:
                store_quarter(0)
                stored = True
        store_quarter(1)
